import numpy as np
import ml_dtypes

BF16 = ml_dtypes.bfloat16


def bf(x):
    return np.asarray(x, np.float32).astype(BF16)


def f32(x):
    return np.asarray(x, np.float32)


def f64(x):
    return np.asarray(x).astype(np.float64)


def striped(idx):
    return np.tile(idx.reshape(-1, 16).T, (8, 1))


D, BIG, C, NN, S, N = 128, 128, 256, 512, 512, 256
TEMP = np.sqrt(C)
SHIFT = np.log(NN)


def setup_inputs():
    return {"base": f32(np.random.standard_normal((C, S))), "target_x": bf(1.5 * np.random.standard_normal((D, N))), "neighbor_x": bf(1.5 * np.random.standard_normal((NN, D))), "neighbor_y": bf(2.0 * np.random.standard_normal((NN, BIG))), "offs": striped(np.random.permutation(S)[:N])}


def reference(base, target_x, neighbor_x, neighbor_y, offs):
    idx = offs[:16].T.reshape(-1)
    tx, nx, ny = f64(target_x), f64(neighbor_x), f64(neighbor_y)
    sim = np.exp(nx @ tx / TEMP - SHIFT)
    degree = 1.0 + sim.sum(axis=0, keepdims=True)
    nf = np.concatenate([nx, ny], axis=1)
    tf = np.concatenate([tx, np.zeros((BIG, N))], axis=0)
    out = f64(base).copy()
    out[:, idx] = (tf + nf.T @ sim) * (1.0 / degree)
    return out

@@ -1,0 +1,75 @@
+import math
+
+import concourse.mybir as mybir
+from concourse.masks import make_identity
+
+BF16, F32, U16 = mybir.dt.bfloat16, mybir.dt.float32, mybir.dt.uint16
+EXP = mybir.ActivationFunctionType.Exp
+COPY = mybir.ActivationFunctionType.Copy
+MULT = mybir.AluOpType.mult
+
+P = 128
+D = 128
+C = 256
+NN = 512
+S = 512
+N = 256
+NB = NN // P
+CB = C // P
+
+FLOPS = 2 * NN * D * N + 2 * NN * C * N
+
+
+def tile_gnn_kernel(tc, base, target_x, neighbor_x, neighbor_y, offs, out):
+    nc = tc.nc
+    with (
+        tc.tile_pool(name="held", bufs=1) as held,
+        tc.psum_pool(name="flip", bufs=2) as flip,
+        tc.psum_pool(name="score", bufs=3) as score,
+        tc.psum_pool(name="sums", bufs=1) as sums,
+    ):
+        nx = held.tile([P, NB, D], BF16, name="nx")
+        ny = held.tile([P, NB, C - D], BF16, name="ny")
+        tx = held.tile([D, N], BF16, name="tx")
+        offsets = held.tile([P, N // 16], U16, name="offsets")
+        windows = [held.tile([P, S], F32, name=f"window{b}") for b in range(CB)]
+        nc.sync.dma_start(nx[:], neighbor_x.rearrange("(p k) d -> p k d", k=NB))
+        nc.scalar.dma_start(tx[:], target_x)
+        nc.scalar.dma_start(ny[:], neighbor_y.rearrange("(p k) d -> p k d", k=NB))
+        nc.sync.dma_start(offsets[:], offs)
+        for b in range(CB):
+            nc.sync.dma_start(windows[b][:], base[b * P : (b + 1) * P, :])
+
+        identity = held.tile([P, P], BF16, name="identity")
+        make_identity(nc, identity[:])
+        ones = held.tile([P, N], BF16, name="ones")
+        nc.vector.memset(ones[:], 1.0)
+
+        message = [sums.tile([P, N], F32, name=f"message{b}") for b in range(CB)]
+        degree = sums.tile([P, N], F32, name="degree")
+        nc.tensor.matmul(message[0][:], identity[:], tx[:], start=True, stop=False)
+        nc.tensor.matmul(degree[:], identity[:], ones[:], start=True, stop=False)
+
+        for k in range(NB):
+            nx_flipped_psum = flip.tile([D, P], BF16, name="nx_flipped_psum")
+            nc.tensor.transpose(nx_flipped_psum[:], nx[:, k, :], identity[:])
+            nx_flipped = held.tile([D, P], BF16, name=f"nx_flipped{k}")
+            nc.vector.tensor_copy(nx_flipped[:], nx_flipped_psum[:])
+
+            dots = score.tile([P, N], F32, name="dots")
+            nc.tensor.matmul(dots[:], nx_flipped[:], tx[:], start=True, stop=True)
+            sim = held.tile([P, N], BF16, name=f"sim{k}")
+            nc.scalar.activation(sim[:], dots[:], EXP, bias=-math.log(NN), scale=1.0 / math.sqrt(C))
+
+            last = k == NB - 1
+            nc.tensor.matmul(degree[:], ones[:, :P], sim[:], start=False, stop=last)
+            nc.tensor.matmul(message[0][:], nx[:, k, :], sim[:], start=False, stop=last)
+            nc.tensor.matmul(message[1][:], ny[:, k, :], sim[:], start=(k == 0), stop=last)
+
+        inverse_degree = held.tile([P, N], F32, name="inverse_degree")
+        nc.vector.reciprocal(inverse_degree[:], degree[:])
+        for b in range(CB):
+            summed = held.tile([P, N], F32, name=f"summed{b}")
+            nc.scalar.activation(summed[:], message[b][:], COPY)
+            nc.vector.tensor_tensor(windows[b][:].indirect(offsets[:]), summed[:], inverse_degree[:], MULT)
+            nc.sync.dma_start(out[b * P : (b + 1) * P, :], windows[b][:])

@@ -45,26 +45,29 @@ def tile_gnn_kernel(tc, base, target_x, neighbor_x, neighbor_y, offs, out):
         ones = held.tile([P, N], BF16, name="ones")
         nc.vector.memset(ones[:], 1.0)
 
+        nx_flipped = [held.tile([D, P], BF16, name=f"nx_flipped{k}") for k in range(NB)]
+        sim = [held.tile([P, N], BF16, name=f"sim{k}") for k in range(NB)]
+        for k in range(NB + 1):
+            if k < NB:
+                nx_flipped_psum = flip.tile([D, P], BF16, name="nx_flipped_psum")
+                nc.tensor.transpose(nx_flipped_psum[:], nx[:, k, :], identity[:])
+                nc.vector.tensor_copy(nx_flipped[k][:], nx_flipped_psum[:])
+            if k > 0:
+                dots = score.tile([P, N], F32, name="dots")
+                nc.tensor.matmul(dots[:], nx_flipped[k - 1][:], tx[:], start=True, stop=True)
+                nc.scalar.activation(
+                    sim[k - 1][:], dots[:], EXP, bias=-math.log(NN), scale=1.0 / math.sqrt(C)
+                )
+
         message = [sums.tile([P, N], F32, name=f"message{b}") for b in range(CB)]
         degree = sums.tile([P, N], F32, name="degree")
-        nc.tensor.matmul(message[0][:], identity[:], tx[:], start=True, stop=False)
         nc.tensor.matmul(degree[:], identity[:], ones[:], start=True, stop=False)
-
+        nc.tensor.matmul(message[0][:], identity[:], tx[:], start=True, stop=False)
         for k in range(NB):
-            nx_flipped_psum = flip.tile([D, P], BF16, name="nx_flipped_psum")
-            nc.tensor.transpose(nx_flipped_psum[:], nx[:, k, :], identity[:])
-            nx_flipped = held.tile([D, P], BF16, name=f"nx_flipped{k}")
-            nc.vector.tensor_copy(nx_flipped[:], nx_flipped_psum[:])
-
-            dots = score.tile([P, N], F32, name="dots")
-            nc.tensor.matmul(dots[:], nx_flipped[:], tx[:], start=True, stop=True)
-            sim = held.tile([P, N], BF16, name=f"sim{k}")
-            nc.scalar.activation(sim[:], dots[:], EXP, bias=-math.log(NN), scale=1.0 / math.sqrt(C))
-
             last = k == NB - 1
-            nc.tensor.matmul(degree[:], ones[:, :P], sim[:], start=False, stop=last)
-            nc.tensor.matmul(message[0][:], nx[:, k, :], sim[:], start=False, stop=last)
-            nc.tensor.matmul(message[1][:], ny[:, k, :], sim[:], start=(k == 0), stop=last)
+            nc.tensor.matmul(degree[:], ones[:, :P], sim[k][:], start=False, stop=last)
+            nc.tensor.matmul(message[0][:], nx[:, k, :], sim[k][:], start=False, stop=last)
+            nc.tensor.matmul(message[1][:], ny[:, k, :], sim[k][:], start=(k == 0), stop=last)
 
         inverse_degree = held.tile([P, N], F32, name="inverse_degree")
         nc.vector.reciprocal(inverse_degree[:], degree[:])

@@ -45,6 +45,10 @@ def tile_gnn_kernel(tc, base, target_x, neighbor_x, neighbor_y, offs, out):
         ones = held.tile([P, N], BF16, name="ones")
         nc.vector.memset(ones[:], 1.0)
 
+        message = [sums.tile([P, N], F32, name=f"message{b}") for b in range(CB)]
+        degree = sums.tile([P, N], F32, name="degree")
+        nc.tensor.matmul(degree[:], identity[:], ones[:], start=True, stop=False)
+
         nx_flipped = [held.tile([D, P], BF16, name=f"nx_flipped{k}") for k in range(NB)]
         sim = [held.tile([P, N], BF16, name=f"sim{k}") for k in range(NB)]
         for k in range(NB + 1):
@@ -59,18 +63,17 @@ def tile_gnn_kernel(tc, base, target_x, neighbor_x, neighbor_y, offs, out):
                     sim[k - 1][:], dots[:], EXP, bias=-math.log(NN), scale=1.0 / math.sqrt(C)
                 )
 
-        message = [sums.tile([P, N], F32, name=f"message{b}") for b in range(CB)]
-        degree = sums.tile([P, N], F32, name="degree")
-        nc.tensor.matmul(degree[:], identity[:], ones[:], start=True, stop=False)
-        nc.tensor.matmul(message[0][:], identity[:], tx[:], start=True, stop=False)
         for k in range(NB):
-            last = k == NB - 1
-            nc.tensor.matmul(degree[:], ones[:, :P], sim[k][:], start=False, stop=last)
-            nc.tensor.matmul(message[0][:], nx[:, k, :], sim[k][:], start=False, stop=last)
-            nc.tensor.matmul(message[1][:], ny[:, k, :], sim[k][:], start=(k == 0), stop=last)
-
+            nc.tensor.matmul(degree[:], ones[:, :P], sim[k][:], start=False, stop=(k == NB - 1))
         inverse_degree = held.tile([P, N], F32, name="inverse_degree")
         nc.vector.reciprocal(inverse_degree[:], degree[:])
+
+        for k in range(NB):
+            nc.tensor.matmul(message[0][:], nx[:, k, :], sim[k][:], start=(k == 0), stop=False)
+        nc.tensor.matmul(message[0][:], identity[:], tx[:], start=False, stop=True)
+        for k in range(NB):
+            nc.tensor.matmul(message[1][:], ny[:, k, :], sim[k][:], start=(k == 0), stop=(k == NB - 1))
+
         for b in range(CB):
             summed = held.tile([P, N], F32, name=f"summed{b}")
             nc.scalar.activation(summed[:], message[b][:], COPY)

@@ -24,9 +24,7 @@ def tile_gnn_kernel(tc, base, target_x, neighbor_x, neighbor_y, offs, out):
     nc = tc.nc
     with (
         tc.tile_pool(name="held", bufs=1) as held,
-        tc.psum_pool(name="flip", bufs=2) as flip,
-        tc.psum_pool(name="score", bufs=3) as score,
-        tc.psum_pool(name="sums", bufs=1) as sums,
+        tc.psum_pool(name="banks", bufs=8) as banks,
     ):
         nx = held.tile([P, NB, D], BF16, name="nx")
         ny = held.tile([P, NB, C - D], BF16, name="ny")
@@ -45,29 +43,27 @@ def tile_gnn_kernel(tc, base, target_x, neighbor_x, neighbor_y, offs, out):
         ones = held.tile([P, N], BF16, name="ones")
         nc.vector.memset(ones[:], 1.0)
 
-        message = [sums.tile([P, N], F32, name=f"message{b}") for b in range(CB)]
-        degree = sums.tile([P, N], F32, name="degree")
-        nc.tensor.matmul(degree[:], identity[:], ones[:], start=True, stop=False)
 
         nx_flipped = [held.tile([D, P], BF16, name=f"nx_flipped{k}") for k in range(NB)]
-        sim = [held.tile([P, N], BF16, name=f"sim{k}") for k in range(NB)]
-        for k in range(NB + 1):
-            if k < NB:
-                nx_flipped_psum = flip.tile([D, P], BF16, name="nx_flipped_psum")
-                nc.tensor.transpose(nx_flipped_psum[:], nx[:, k, :], identity[:])
-                nc.vector.tensor_copy(nx_flipped[k][:], nx_flipped_psum[:])
-            if k > 0:
-                dots = score.tile([P, N], F32, name="dots")
-                nc.tensor.matmul(dots[:], nx_flipped[k - 1][:], tx[:], start=True, stop=True)
-                nc.scalar.activation(
-                    sim[k - 1][:], dots[:], EXP, bias=-math.log(NN), scale=1.0 / math.sqrt(C)
-                )
+        for k in range(NB):
+            nx_flipped_psum = banks.tile([D, P], BF16, name="nx_flipped_psum", tag="bank")
+            nc.tensor.matmul(nx_flipped_psum[:], nx[:, k, :], identity[:], start=True, stop=True)
+            nc.vector.tensor_copy(nx_flipped[k][:], nx_flipped_psum[:])
 
+        sim = [held.tile([P, N], BF16, name=f"sim{k}") for k in range(NB)]
+        for k in range(NB):
+            dots = banks.tile([P, N], F32, name="dots", tag="bank")
+            nc.tensor.matmul(dots[:], nx_flipped[k][:], tx[:], start=True, stop=True)
+            nc.scalar.activation(sim[k][:], dots[:], EXP, bias=-math.log(NN), scale=1.0 / math.sqrt(C))
+
+        degree = banks.tile([P, N], F32, name="degree", tag="bank")
+        nc.tensor.matmul(degree[:], identity[:], ones[:], start=True, stop=False)
         for k in range(NB):
             nc.tensor.matmul(degree[:], ones[:, :P], sim[k][:], start=False, stop=(k == NB - 1))
         inverse_degree = held.tile([P, N], F32, name="inverse_degree")
         nc.vector.reciprocal(inverse_degree[:], degree[:])
 
+        message = [banks.tile([P, N], F32, name=f"message{b}", tag="bank") for b in range(CB)]
         for k in range(NB):
             nc.tensor.matmul(message[0][:], nx[:, k, :], sim[k][:], start=(k == 0), stop=False)
         nc.tensor.matmul(message[0][:], identity[:], tx[:], start=False, stop=True)

@@ -32,8 +32,8 @@ def tile_gnn_kernel(tc, base, target_x, neighbor_x, neighbor_y, offs, out):
         offsets = held.tile([P, N // 16], U16, name="offsets")
         windows = [held.tile([P, S], F32, name=f"window{b}") for b in range(CB)]
         nc.sync.dma_start(nx[:], neighbor_x.rearrange("(p k) d -> p k d", k=NB))
-        nc.scalar.dma_start(tx[:], target_x)
-        nc.scalar.dma_start(ny[:], neighbor_y.rearrange("(p k) d -> p k d", k=NB))
+        nc.sync.dma_start(tx[:], target_x)
+        nc.sync.dma_start(ny[:], neighbor_y.rearrange("(p k) d -> p k d", k=NB))
         nc.sync.dma_start(offsets[:], offs)
         for b in range(CB):
             nc.sync.dma_start(windows[b][:], base[b * P : (b + 1) * P, :])

@@ -16,6 +16,7 @@ S = 512
 N = 256
 NB = NN // P
 CB = C // P
+HALVES = 2
 
 FLOPS = 2 * NN * D * N + 2 * NN * C * N
 
@@ -51,17 +52,22 @@ def tile_gnn_kernel(tc, base, target_x, neighbor_x, neighbor_y, offs, out):
             nc.vector.tensor_copy(nx_flipped[k][:], nx_flipped_psum[:])
 
         sim = [held.tile([P, N], BF16, name=f"sim{k}") for k in range(NB)]
+        dots = [banks.tile([P, N], F32, name=f"dots{k}", tag="bank") for k in range(NB)]
         for k in range(NB):
-            dots = banks.tile([P, N], F32, name="dots", tag="bank")
-            nc.tensor.matmul(dots[:], nx_flipped[k][:], tx[:], start=True, stop=True)
-            nc.scalar.activation(sim[k][:], dots[:], EXP, bias=-math.log(NN), scale=1.0 / math.sqrt(C))
+            nc.tensor.matmul(dots[k][:], nx_flipped[k][:], tx[:], start=True, stop=True)
 
-        degree = banks.tile([P, N], F32, name="degree", tag="bank")
-        nc.tensor.matmul(degree[:], identity[:], ones[:], start=True, stop=False)
-        for k in range(NB):
-            nc.tensor.matmul(degree[:], ones[:, :P], sim[k][:], start=False, stop=(k == NB - 1))
         inverse_degree = held.tile([P, N], F32, name="inverse_degree")
-        nc.vector.reciprocal(inverse_degree[:], degree[:])
+        for h in range(HALVES):
+            part = slice(h * (N // HALVES), (h + 1) * (N // HALVES))
+            for k in range(NB):
+                nc.scalar.activation(
+                    sim[k][:, part], dots[k][:, part], EXP, bias=-math.log(NN), scale=1.0 / math.sqrt(C)
+                )
+            degree = banks.tile([P, N // HALVES], F32, name="degree", tag="bank")
+            nc.tensor.matmul(degree[:], identity[:], ones[:, part], start=True, stop=False)
+            for k in range(NB):
+                nc.tensor.matmul(degree[:], ones[:, :P], sim[k][:, part], start=False, stop=(k == NB - 1))
+            nc.vector.reciprocal(inverse_degree[:, part], degree[:])
 
         message = [banks.tile([P, N], F32, name=f"message{b}", tag="bank") for b in range(CB)]
         for k in range(NB):

@@ -16,7 +16,8 @@ S = 512
 N = 256
 NB = NN // P
 CB = C // P
-HALVES = 2
+PARTS = 4
+NP = N // PARTS
 
 FLOPS = 2 * NN * D * N + 2 * NN * C * N
 
@@ -41,7 +42,7 @@ def tile_gnn_kernel(tc, base, target_x, neighbor_x, neighbor_y, offs, out):
 
         identity = held.tile([P, P], BF16, name="identity")
         make_identity(nc, identity[:])
-        ones = held.tile([P, N], BF16, name="ones")
+        ones = held.tile([P, P], BF16, name="ones")
         nc.vector.memset(ones[:], 1.0)
 
 
@@ -51,33 +52,36 @@ def tile_gnn_kernel(tc, base, target_x, neighbor_x, neighbor_y, offs, out):
             nc.tensor.matmul(nx_flipped_psum[:], nx[:, k, :], identity[:], start=True, stop=True)
             nc.vector.tensor_copy(nx_flipped[k][:], nx_flipped_psum[:])
 
-        sim = [held.tile([P, N], BF16, name=f"sim{k}") for k in range(NB)]
-        dots = [banks.tile([P, N], F32, name=f"dots{k}", tag="bank") for k in range(NB)]
-        for k in range(NB):
-            nc.tensor.matmul(dots[k][:], nx_flipped[k][:], tx[:], start=True, stop=True)
+        columns = [slice(q * NP, (q + 1) * NP) for q in range(PARTS)]
 
-        inverse_degree = held.tile([P, N], F32, name="inverse_degree")
-        for h in range(HALVES):
-            part = slice(h * (N // HALVES), (h + 1) * (N // HALVES))
+        sim = []
+        for q in range(PARTS):
+            dots = banks.tile([P, NB, NP], F32, name=f"dots{q}", tag="bank")
             for k in range(NB):
-                nc.scalar.activation(
-                    sim[k][:, part], dots[k][:, part], EXP, bias=-math.log(NN), scale=1.0 / math.sqrt(C)
-                )
-            degree = banks.tile([P, N // HALVES], F32, name="degree", tag="bank")
-            nc.tensor.matmul(degree[:], identity[:], ones[:, part], start=True, stop=False)
+                nc.tensor.matmul(dots[:, k, :], nx_flipped[k][:], tx[:, columns[q]], start=True, stop=True)
+            sim.append(held.tile([P, NB, NP], BF16, name=f"sim{q}"))
+            nc.scalar.activation(sim[q][:], dots[:], EXP, bias=-math.log(NN), scale=1.0 / math.sqrt(C))
+
+        inverse_degree = []
+        for q in range(PARTS):
+            degree = banks.tile([P, NP], F32, name=f"degree{q}", tag="bank")
+            nc.tensor.matmul(degree[:], identity[:], ones[:, :NP], start=True, stop=False)
             for k in range(NB):
-                nc.tensor.matmul(degree[:], ones[:, :P], sim[k][:, part], start=False, stop=(k == NB - 1))
-            nc.vector.reciprocal(inverse_degree[:, part], degree[:])
+                nc.tensor.matmul(degree[:], ones[:], sim[q][:, k, :], start=False, stop=(k == NB - 1))
+            inverse_degree.append(held.tile([P, NP], F32, name=f"inverse_degree{q}"))
+            nc.vector.reciprocal(inverse_degree[q][:], degree[:])
 
-        message = [banks.tile([P, N], F32, name=f"message{b}", tag="bank") for b in range(CB)]
-        for k in range(NB):
-            nc.tensor.matmul(message[0][:], nx[:, k, :], sim[k][:], start=(k == 0), stop=False)
-        nc.tensor.matmul(message[0][:], identity[:], tx[:], start=False, stop=True)
-        for k in range(NB):
-            nc.tensor.matmul(message[1][:], ny[:, k, :], sim[k][:], start=(k == 0), stop=(k == NB - 1))
-
+        for q in range(PARTS):
+            message = banks.tile([P, CB, NP], F32, name=f"message{q}", tag="bank")
+            nc.tensor.matmul(message[:, 0, :], identity[:], tx[:, columns[q]], start=True, stop=False)
+            for k in range(NB):
+                nc.tensor.matmul(message[:, 0, :], nx[:, k, :], sim[q][:, k, :], start=False, stop=(k == NB - 1))
+            for k in range(NB):
+                nc.tensor.matmul(message[:, 1, :], ny[:, k, :], sim[q][:, k, :], start=(k == 0), stop=(k == NB - 1))
+            summed = held.tile([P, CB, NP], F32, name=f"summed{q}")
+            nc.scalar.activation(summed[:], message[:], COPY)
+            entries = offsets[:, q * (NP // 16) : (q + 1) * (NP // 16)]
+            for b in range(CB):
+                nc.vector.tensor_tensor(windows[b][:].indirect(entries), summed[:, b, :], inverse_degree[q][:], MULT)
         for b in range(CB):
-            summed = held.tile([P, N], F32, name=f"summed{b}")
-            nc.scalar.activation(summed[:], message[b][:], COPY)
-            nc.vector.tensor_tensor(windows[b][:].indirect(offsets[:]), summed[:], inverse_degree[:], MULT)
             nc.sync.dma_start(out[b * P : (b + 1) * P, :], windows[b][:])

@@ -16,7 +16,7 @@ S = 512
 N = 256
 NB = NN // P
 CB = C // P
-PARTS = 4
+PARTS = 2
 NP = N // PARTS
 
 FLOPS = 2 * NN * D * N + 2 * NN * C * N
@@ -42,8 +42,10 @@ def tile_gnn_kernel(tc, base, target_x, neighbor_x, neighbor_y, offs, out):
 
         identity = held.tile([P, P], BF16, name="identity")
         make_identity(nc, identity[:])
-        ones = held.tile([P, P], BF16, name="ones")
-        nc.vector.memset(ones[:], 1.0)
+        identity_f32 = held.tile([P, P], F32, name="identity_f32")
+        make_identity(nc, identity_f32[:])
+        one = held.tile([P, 1], BF16, name="one")
+        nc.vector.memset(one[:], 1.0)
 
 
         nx_flipped = [held.tile([D, P], BF16, name=f"nx_flipped{k}") for k in range(NB)]
@@ -62,26 +64,40 @@ def tile_gnn_kernel(tc, base, target_x, neighbor_x, neighbor_y, offs, out):
             sim.append(held.tile([P, NB, NP], BF16, name=f"sim{q}"))
             nc.scalar.activation(sim[q][:], dots[:], EXP, bias=-math.log(NN), scale=1.0 / math.sqrt(C))
 
-        inverse_degree = []
+        message = [[banks.tile([P, NP], F32, name=f"message{b}_{q}", tag="bank") for b in range(CB)] for q in range(PARTS)]
+        degree = [banks.tile([NP, 1], F32, name=f"degree{q}", tag="bank") for q in range(PARTS)]
         for q in range(PARTS):
-            degree = banks.tile([P, NP], F32, name=f"degree{q}", tag="bank")
-            nc.tensor.matmul(degree[:], identity[:], ones[:, :NP], start=True, stop=False)
-            for k in range(NB):
-                nc.tensor.matmul(degree[:], ones[:], sim[q][:, k, :], start=False, stop=(k == NB - 1))
-            inverse_degree.append(held.tile([P, NP], F32, name=f"inverse_degree{q}"))
-            nc.vector.reciprocal(inverse_degree[q][:], degree[:])
+            nc.tensor.matmul(message[q][0][:], identity[:], tx[:, columns[q]], start=True, stop=False)
+            nc.tensor.matmul(degree[q][:], identity[:, :NP], one[:], start=True, stop=False)
 
+        inverse_column = [held.tile([NP, 1], F32, name=f"inverse_column{q}") for q in range(PARTS)]
+
+        def invert_degree(q):
+            for k in range(NB):
+                nc.tensor.matmul(degree[q][:], sim[q][:, k, :], one[:], start=False, stop=(k == NB - 1))
+            nc.vector.reciprocal(inverse_column[q][:], degree[q][:])
+
+        invert_degree(0)
         for q in range(PARTS):
-            message = banks.tile([P, CB, NP], F32, name=f"message{q}", tag="bank")
-            nc.tensor.matmul(message[:, 0, :], identity[:], tx[:, columns[q]], start=True, stop=False)
+            summed = [held.tile([P, NP], F32, name=f"summed{b}_{q}") for b in range(CB)]
             for k in range(NB):
-                nc.tensor.matmul(message[:, 0, :], nx[:, k, :], sim[q][:, k, :], start=False, stop=(k == NB - 1))
+                nc.tensor.matmul(message[q][0][:], nx[:, k, :], sim[q][:, k, :], start=False, stop=(k == NB - 1))
+            nc.scalar.activation(summed[0][:], message[q][0][:], COPY)
+
+            inverse_rows = banks.tile([P, NP], F32, name=f"inverse_rows{q}", tag="bank")
+            nc.tensor.transpose(inverse_rows[:], inverse_column[q][:].to_broadcast([NP, P]), identity_f32[:NP, :NP])
+            inverse_degree = held.tile([P, NP], F32, name=f"inverse_degree{q}")
+            nc.scalar.activation(inverse_degree[:], inverse_rows[:], COPY)
+
+            if q + 1 < PARTS:
+                invert_degree(q + 1)
+
             for k in range(NB):
-                nc.tensor.matmul(message[:, 1, :], ny[:, k, :], sim[q][:, k, :], start=(k == 0), stop=(k == NB - 1))
-            summed = held.tile([P, CB, NP], F32, name=f"summed{q}")
-            nc.scalar.activation(summed[:], message[:], COPY)
+                nc.tensor.matmul(message[q][1][:], ny[:, k, :], sim[q][:, k, :], start=(k == 0), stop=(k == NB - 1))
+            nc.scalar.activation(summed[1][:], message[q][1][:], COPY)
+
             entries = offsets[:, q * (NP // 16) : (q + 1) * (NP // 16)]
             for b in range(CB):
-                nc.vector.tensor_tensor(windows[b][:].indirect(entries), summed[:, b, :], inverse_degree[q][:], MULT)
+                nc.vector.tensor_tensor(windows[b][:].indirect(entries), summed[b][:], inverse_degree[:], MULT)
         for b in range(CB):
             nc.sync.dma_start(out[b * P : (b + 1) * P, :], windows[b][:])

@@ -56,19 +56,21 @@ def tile_gnn_kernel(tc, base, target_x, neighbor_x, neighbor_y, offs, out):
 
         columns = [slice(q * NP, (q + 1) * NP) for q in range(PARTS)]
 
-        sim = []
+        dots = [banks.tile([P, N], F32, name=f"dots{k}", tag="bank") for k in range(NB)]
+        for k in range(NB):
+            nc.tensor.matmul(dots[k][:], nx_flipped[k][:], tx[:], start=True, stop=True)
+        sim = [held.tile([P, NB, NP], BF16, name=f"sim{q}") for q in range(PARTS)]
         for q in range(PARTS):
-            dots = banks.tile([P, NB, NP], F32, name=f"dots{q}", tag="bank")
             for k in range(NB):
-                nc.tensor.matmul(dots[:, k, :], nx_flipped[k][:], tx[:, columns[q]], start=True, stop=True)
-            sim.append(held.tile([P, NB, NP], BF16, name=f"sim{q}"))
-            nc.scalar.activation(sim[q][:], dots[:], EXP, bias=-math.log(NN), scale=1.0 / math.sqrt(C))
+                nc.scalar.activation(
+                    sim[q][:, k, :], dots[k][:, columns[q]], EXP, bias=-math.log(NN), scale=1.0 / math.sqrt(C)
+                )
 
-        message = [[banks.tile([P, NP], F32, name=f"message{b}_{q}", tag="bank") for b in range(CB)] for q in range(PARTS)]
         degree = [banks.tile([NP, 1], F32, name=f"degree{q}", tag="bank") for q in range(PARTS)]
+        message = [[banks.tile([P, NP], F32, name=f"message{b}_{q}", tag="bank") for q in range(PARTS)] for b in range(CB)]
         for q in range(PARTS):
-            nc.tensor.matmul(message[q][0][:], identity[:], tx[:, columns[q]], start=True, stop=False)
             nc.tensor.matmul(degree[q][:], identity[:, :NP], one[:], start=True, stop=False)
+            nc.tensor.matmul(message[0][q][:], identity[:], tx[:, columns[q]], start=True, stop=False)
 
         inverse_column = [held.tile([NP, 1], F32, name=f"inverse_column{q}") for q in range(PARTS)]
 
@@ -81,8 +83,8 @@ def tile_gnn_kernel(tc, base, target_x, neighbor_x, neighbor_y, offs, out):
         for q in range(PARTS):
             summed = [held.tile([P, NP], F32, name=f"summed{b}_{q}") for b in range(CB)]
             for k in range(NB):
-                nc.tensor.matmul(message[q][0][:], nx[:, k, :], sim[q][:, k, :], start=False, stop=(k == NB - 1))
-            nc.scalar.activation(summed[0][:], message[q][0][:], COPY)
+                nc.tensor.matmul(message[0][q][:], nx[:, k, :], sim[q][:, k, :], start=False, stop=(k == NB - 1))
+            nc.scalar.activation(summed[0][:], message[0][q][:], COPY)
 
             inverse_rows = banks.tile([P, NP], F32, name=f"inverse_rows{q}", tag="bank")
             nc.tensor.transpose(inverse_rows[:], inverse_column[q][:].to_broadcast([NP, P]), identity_f32[:NP, :NP])
@@ -93,8 +95,8 @@ def tile_gnn_kernel(tc, base, target_x, neighbor_x, neighbor_y, offs, out):
                 invert_degree(q + 1)
 
             for k in range(NB):
-                nc.tensor.matmul(message[q][1][:], ny[:, k, :], sim[q][:, k, :], start=(k == 0), stop=(k == NB - 1))
-            nc.scalar.activation(summed[1][:], message[q][1][:], COPY)
+                nc.tensor.matmul(message[1][q][:], ny[:, k, :], sim[q][:, k, :], start=(k == 0), stop=(k == NB - 1))
+            nc.scalar.activation(summed[1][:], message[1][q][:], COPY)
 
             entries = offsets[:, q * (NP // 16) : (q + 1) * (NP // 16)]
             for b in range(CB):

@@ -56,15 +56,12 @@ def tile_gnn_kernel(tc, base, target_x, neighbor_x, neighbor_y, offs, out):
 
         columns = [slice(q * NP, (q + 1) * NP) for q in range(PARTS)]
 
-        dots = [banks.tile([P, N], F32, name=f"dots{k}", tag="bank") for k in range(NB)]
-        for k in range(NB):
-            nc.tensor.matmul(dots[k][:], nx_flipped[k][:], tx[:], start=True, stop=True)
         sim = [held.tile([P, NB, NP], BF16, name=f"sim{q}") for q in range(PARTS)]
         for q in range(PARTS):
             for k in range(NB):
-                nc.scalar.activation(
-                    sim[q][:, k, :], dots[k][:, columns[q]], EXP, bias=-math.log(NN), scale=1.0 / math.sqrt(C)
-                )
+                dots = banks.tile([P, NP], F32, name=f"dots{k}_{q}", tag="bank")
+                nc.tensor.matmul(dots[:], nx_flipped[k][:], tx[:, columns[q]], start=True, stop=True)
+                nc.scalar.activation(sim[q][:, k, :], dots[:], EXP, bias=-math.log(NN), scale=1.0 / math.sqrt(C))
 
         degree = [banks.tile([NP, 1], F32, name=f"degree{q}", tag="bank") for q in range(PARTS)]
         message = [[banks.tile([P, NP], F32, name=f"message{b}_{q}", tag="bank") for q in range(PARTS)] for b in range(CB)]

@@ -43,7 +43,7 @@ def tile_gnn_kernel(tc, base, target_x, neighbor_x, neighbor_y, offs, out):
         identity = held.tile([P, P], BF16, name="identity")
         make_identity(nc, identity[:])
         identity_f32 = held.tile([P, P], F32, name="identity_f32")
-        make_identity(nc, identity_f32[:])
+        nc.scalar.activation(identity_f32[:], identity[:], COPY)
         one = held.tile([P, 1], BF16, name="one")
         nc.vector.memset(one[:], 1.0)
 

@@ -16,8 +16,8 @@ S = 512
 N = 256
 NB = NN // P
 CB = C // P
-PARTS = 2
-NP = N // PARTS
+WIDTHS = (64, 64, 128)
+PARTS = len(WIDTHS)
 
 FLOPS = 2 * NN * D * N + 2 * NN * C * N
 
@@ -44,8 +44,8 @@ def tile_gnn_kernel(tc, base, target_x, neighbor_x, neighbor_y, offs, out):
         make_identity(nc, identity[:])
         identity_f32 = held.tile([P, P], F32, name="identity_f32")
         nc.scalar.activation(identity_f32[:], identity[:], COPY)
-        one = held.tile([P, 1], BF16, name="one")
-        nc.vector.memset(one[:], 1.0)
+        ones = held.tile([P, P], BF16, name="ones")
+        nc.vector.memset(ones[:], 1.0)
 
 
         nx_flipped = [held.tile([D, P], BF16, name=f"nx_flipped{k}") for k in range(NB)]
@@ -54,49 +54,72 @@ def tile_gnn_kernel(tc, base, target_x, neighbor_x, neighbor_y, offs, out):
             nc.tensor.matmul(nx_flipped_psum[:], nx[:, k, :], identity[:], start=True, stop=True)
             nc.vector.tensor_copy(nx_flipped[k][:], nx_flipped_psum[:])
 
-        columns = [slice(q * NP, (q + 1) * NP) for q in range(PARTS)]
+        starts = [sum(WIDTHS[:q]) for q in range(PARTS)]
+        columns = [slice(starts[q], starts[q] + WIDTHS[q]) for q in range(PARTS)]
+        sim = [held.tile([P, NB, w], BF16, name=f"sim{q}") for q, w in enumerate(WIDTHS)]
+        inverse_degree = [held.tile([P, w], F32, name=f"inverse_degree{q}") for q, w in enumerate(WIDTHS)]
+        inverse_column = {}
+        summed = [[held.tile([P, w], F32, name=f"summed{b}_{q}") for b in range(CB)] for q, w in enumerate(WIDTHS)]
 
-        sim = [held.tile([P, NB, NP], BF16, name=f"sim{q}") for q in range(PARTS)]
-        for q in range(PARTS):
+        def similarities(q):
             for k in range(NB):
-                dots = banks.tile([P, NP], F32, name=f"dots{k}_{q}", tag="bank")
+                dots = banks.tile([P, WIDTHS[q]], F32, name=f"dots{k}_{q}", tag="bank")
                 nc.tensor.matmul(dots[:], nx_flipped[k][:], tx[:, columns[q]], start=True, stop=True)
                 nc.scalar.activation(sim[q][:, k, :], dots[:], EXP, bias=-math.log(NN), scale=1.0 / math.sqrt(C))
 
-        degree = [banks.tile([NP, 1], F32, name=f"degree{q}", tag="bank") for q in range(PARTS)]
-        message = [[banks.tile([P, NP], F32, name=f"message{b}_{q}", tag="bank") for q in range(PARTS)] for b in range(CB)]
+        def degree_in_rows(q):
+            degree_rows = banks.tile([P, WIDTHS[q]], F32, name=f"degree_rows{q}", tag="bank")
+            nc.tensor.matmul(degree_rows[:], identity[:], ones[:, : WIDTHS[q]], start=True, stop=False)
+            for k in range(NB):
+                nc.tensor.matmul(degree_rows[:], ones[:], sim[q][:, k, :], start=False, stop=(k == NB - 1))
+            return degree_rows
+
+        def invert_in_column(q):
+            degree = banks.tile([WIDTHS[q], 1], F32, name=f"degree{q}", tag="bank")
+            nc.tensor.matmul(degree[:], identity[:, : WIDTHS[q]], ones[:, :1], start=True, stop=False)
+            for k in range(NB):
+                nc.tensor.matmul(degree[:], sim[q][:, k, :], ones[:, :1], start=False, stop=(k == NB - 1))
+            inverse_column[q] = held.tile([WIDTHS[q], 1], F32, name=f"inverse_column{q}")
+            nc.vector.reciprocal(inverse_column[q][:], degree[:])
+
+        def spread_column(q):
+            w = WIDTHS[q]
+            inverse_rows = banks.tile([P, w], F32, name=f"inverse_rows{q}", tag="bank")
+            nc.tensor.transpose(inverse_rows[:], inverse_column[q][:].to_broadcast([w, P]), identity_f32[:w, :w])
+            nc.scalar.activation(inverse_degree[q][:], inverse_rows[:], COPY)
+
+        self_loop = [banks.tile([P, w], F32, name=f"self_loop{q}", tag="bank") for q, w in enumerate(WIDTHS)]
         for q in range(PARTS):
-            nc.tensor.matmul(degree[q][:], identity[:, :NP], one[:], start=True, stop=False)
-            nc.tensor.matmul(message[0][q][:], identity[:], tx[:, columns[q]], start=True, stop=False)
+            nc.tensor.matmul(self_loop[q][:], identity[:], tx[:, columns[q]], start=True, stop=False)
 
-        inverse_column = [held.tile([NP, 1], F32, name=f"inverse_column{q}") for q in range(PARTS)]
-
-        def invert_degree(q):
+        def messages(q, b):
+            if b == 0:
+                nf, message = nx, self_loop[q]
+            else:
+                nf, message = ny, banks.tile([P, WIDTHS[q]], F32, name=f"message{q}", tag="bank")
             for k in range(NB):
-                nc.tensor.matmul(degree[q][:], sim[q][:, k, :], one[:], start=False, stop=(k == NB - 1))
-            nc.vector.reciprocal(inverse_column[q][:], degree[q][:])
+                nc.tensor.matmul(message[:], nf[:, k, :], sim[q][:, k, :], start=(b > 0 and k == 0), stop=(k == NB - 1))
+            nc.scalar.activation(summed[q][b][:], message[:], COPY)
 
-        invert_degree(0)
-        for q in range(PARTS):
-            summed = [held.tile([P, NP], F32, name=f"summed{b}_{q}") for b in range(CB)]
-            for k in range(NB):
-                nc.tensor.matmul(message[0][q][:], nx[:, k, :], sim[q][:, k, :], start=False, stop=(k == NB - 1))
-            nc.scalar.activation(summed[0][:], message[0][q][:], COPY)
+        def scatter(q, b):
+            entries = offsets[:, starts[q] // 16 : (starts[q] + WIDTHS[q]) // 16]
+            nc.vector.tensor_tensor(windows[b][:].indirect(entries), summed[q][b][:], inverse_degree[q][:], MULT)
 
-            inverse_rows = banks.tile([P, NP], F32, name=f"inverse_rows{q}", tag="bank")
-            nc.tensor.transpose(inverse_rows[:], inverse_column[q][:].to_broadcast([NP, P]), identity_f32[:NP, :NP])
-            inverse_degree = held.tile([P, NP], F32, name=f"inverse_degree{q}")
-            nc.scalar.activation(inverse_degree[:], inverse_rows[:], COPY)
-
-            if q + 1 < PARTS:
-                invert_degree(q + 1)
-
-            for k in range(NB):
-                nc.tensor.matmul(message[1][q][:], ny[:, k, :], sim[q][:, k, :], start=(k == 0), stop=(k == NB - 1))
-            nc.scalar.activation(summed[1][:], message[1][q][:], COPY)
-
-            entries = offsets[:, q * (NP // 16) : (q + 1) * (NP // 16)]
-            for b in range(CB):
-                nc.vector.tensor_tensor(windows[b][:].indirect(entries), summed[b][:], inverse_degree[:], MULT)
+        similarities(0)
+        nc.vector.reciprocal(inverse_degree[0][:], degree_in_rows(0)[:])
+        similarities(1)
+        messages(0, 0)
+        scatter(0, 0)
+        similarities(2)
+        nc.vector.reciprocal(inverse_degree[1][:], degree_in_rows(1)[:])
+        messages(0, 1)
+        scatter(0, 1)
+        invert_in_column(2)
         for b in range(CB):
+            messages(1, b)
+            scatter(1, b)
+        spread_column(2)
+        for b in range(CB):
+            messages(2, b)
+            scatter(2, b)
             nc.sync.dma_start(out[b * P : (b + 1) * P, :], windows[b][:])

@@ -16,7 +16,7 @@ S = 512
 N = 256
 NB = NN // P
 CB = C // P
-WIDTHS = (64, 64, 128)
+WIDTHS = (128, 128)
 PARTS = len(WIDTHS)
 
 FLOPS = 2 * NN * D * N + 2 * NN * C * N
@@ -44,9 +44,13 @@ def tile_gnn_kernel(tc, base, target_x, neighbor_x, neighbor_y, offs, out):
         make_identity(nc, identity[:])
         identity_f32 = held.tile([P, P], F32, name="identity_f32")
         nc.scalar.activation(identity_f32[:], identity[:], COPY)
-        ones = held.tile([P, P], BF16, name="ones")
-        nc.vector.memset(ones[:], 1.0)
+        one = held.tile([P, 1], BF16, name="one")
+        nc.vector.memset(one[:], 1.0)
 
+
+        degree = [banks.tile([w, 1], F32, name=f"degree{q}", tag="bank") for q, w in enumerate(WIDTHS)]
+        for q, w in enumerate(WIDTHS):
+            nc.tensor.matmul(degree[q][:], identity[:, :w], one[:], start=True, stop=False)
 
         nx_flipped = [held.tile([D, P], BF16, name=f"nx_flipped{k}") for k in range(NB)]
         for k in range(NB):
@@ -61,35 +65,30 @@ def tile_gnn_kernel(tc, base, target_x, neighbor_x, neighbor_y, offs, out):
         inverse_column = {}
         summed = [[held.tile([P, w], F32, name=f"summed{b}_{q}") for b in range(CB)] for q, w in enumerate(WIDTHS)]
 
-        def similarities(q):
-            for k in range(NB):
-                dots = banks.tile([P, WIDTHS[q]], F32, name=f"dots{k}_{q}", tag="bank")
-                nc.tensor.matmul(dots[:], nx_flipped[k][:], tx[:, columns[q]], start=True, stop=True)
-                nc.scalar.activation(sim[q][:, k, :], dots[:], EXP, bias=-math.log(NN), scale=1.0 / math.sqrt(C))
+        def similarities(q, blocks_a_bank):
+            for first in range(0, NB, blocks_a_bank):
+                blocks = slice(first, first + blocks_a_bank)
+                dots = banks.tile([P, blocks_a_bank, WIDTHS[q]], F32, name=f"dots{first}_{q}", tag="bank")
+                for i in range(blocks_a_bank):
+                    nc.tensor.matmul(dots[:, i, :], nx_flipped[first + i][:], tx[:, columns[q]], start=True, stop=True)
+                nc.scalar.activation(sim[q][:, blocks, :], dots[:], EXP, bias=-math.log(NN), scale=1.0 / math.sqrt(C))
 
-        def degree_in_rows(q):
-            degree_rows = banks.tile([P, WIDTHS[q]], F32, name=f"degree_rows{q}", tag="bank")
-            nc.tensor.matmul(degree_rows[:], identity[:], ones[:, : WIDTHS[q]], start=True, stop=False)
+        def invert_degree(q):
             for k in range(NB):
-                nc.tensor.matmul(degree_rows[:], ones[:], sim[q][:, k, :], start=False, stop=(k == NB - 1))
-            return degree_rows
-
-        def invert_in_column(q):
-            degree = banks.tile([WIDTHS[q], 1], F32, name=f"degree{q}", tag="bank")
-            nc.tensor.matmul(degree[:], identity[:, : WIDTHS[q]], ones[:, :1], start=True, stop=False)
-            for k in range(NB):
-                nc.tensor.matmul(degree[:], sim[q][:, k, :], ones[:, :1], start=False, stop=(k == NB - 1))
+                nc.tensor.matmul(degree[q][:], sim[q][:, k, :], one[:], start=False, stop=(k == NB - 1))
             inverse_column[q] = held.tile([WIDTHS[q], 1], F32, name=f"inverse_column{q}")
-            nc.vector.reciprocal(inverse_column[q][:], degree[:])
+            nc.vector.reciprocal(inverse_column[q][:], degree[q][:])
 
-        def spread_column(q):
+        def spread_inverse(q):
             w = WIDTHS[q]
             inverse_rows = banks.tile([P, w], F32, name=f"inverse_rows{q}", tag="bank")
             nc.tensor.transpose(inverse_rows[:], inverse_column[q][:].to_broadcast([w, P]), identity_f32[:w, :w])
             nc.scalar.activation(inverse_degree[q][:], inverse_rows[:], COPY)
 
-        self_loop = [banks.tile([P, w], F32, name=f"self_loop{q}", tag="bank") for q, w in enumerate(WIDTHS)]
-        for q in range(PARTS):
+        self_loop = {}
+
+        def open_with_self_loop(q):
+            self_loop[q] = banks.tile([P, WIDTHS[q]], F32, name=f"self_loop{q}", tag="bank")
             nc.tensor.matmul(self_loop[q][:], identity[:], tx[:, columns[q]], start=True, stop=False)
 
         def messages(q, b):
@@ -105,21 +104,20 @@ def tile_gnn_kernel(tc, base, target_x, neighbor_x, neighbor_y, offs, out):
             entries = offsets[:, starts[q] // 16 : (starts[q] + WIDTHS[q]) // 16]
             nc.vector.tensor_tensor(windows[b][:].indirect(entries), summed[q][b][:], inverse_degree[q][:], MULT)
 
-        similarities(0)
-        nc.vector.reciprocal(inverse_degree[0][:], degree_in_rows(0)[:])
-        similarities(1)
+        open_with_self_loop(0)
+        similarities(0, blocks_a_bank=1)
+        similarities(1, blocks_a_bank=1)
+        invert_degree(0)
         messages(0, 0)
-        scatter(0, 0)
-        similarities(2)
-        nc.vector.reciprocal(inverse_degree[1][:], degree_in_rows(1)[:])
+        spread_inverse(0)
+        invert_degree(1)
         messages(0, 1)
-        scatter(0, 1)
-        invert_in_column(2)
         for b in range(CB):
-            messages(1, b)
+            scatter(0, b)
+        open_with_self_loop(1)
+        messages(1, 0)
+        spread_inverse(1)
+        messages(1, 1)
+        for b in range(CB):
             scatter(1, b)
-        spread_column(2)
-        for b in range(CB):
-            messages(2, b)
-            scatter(2, b)
             nc.sync.dma_start(out[b * P : (b + 1) * P, :], windows[b][:])

@@ -35,10 +35,10 @@ def tile_gnn_kernel(tc, base, target_x, neighbor_x, neighbor_y, offs, out):
         windows = [held.tile([P, S], F32, name=f"window{b}") for b in range(CB)]
         nc.sync.dma_start(nx[:], neighbor_x.rearrange("(p k) d -> p k d", k=NB))
         nc.sync.dma_start(tx[:], target_x)
-        nc.sync.dma_start(ny[:], neighbor_y.rearrange("(p k) d -> p k d", k=NB))
         nc.sync.dma_start(offsets[:], offs)
-        for b in range(CB):
-            nc.sync.dma_start(windows[b][:], base[b * P : (b + 1) * P, :])
+        nc.sync.dma_start(windows[0][:], base[:P, :])
+        nc.sync.dma_start(ny[:], neighbor_y.rearrange("(p k) d -> p k d", k=NB))
+        nc.sync.dma_start(windows[1][:], base[P:, :])
 
         identity = held.tile([P, P], BF16, name="identity")
         make_identity(nc, identity[:])

@@ -48,9 +48,13 @@ def tile_gnn_kernel(tc, base, target_x, neighbor_x, neighbor_y, offs, out):
         nc.vector.memset(one[:], 1.0)
 
 
-        degree = [banks.tile([w, 1], F32, name=f"degree{q}", tag="bank") for q, w in enumerate(WIDTHS)]
-        for q, w in enumerate(WIDTHS):
-            nc.tensor.matmul(degree[q][:], identity[:, :w], one[:], start=True, stop=False)
+        degree = {}
+
+        def open_degree(q):
+            degree[q] = banks.tile([WIDTHS[q], 1], F32, name=f"degree{q}", tag="bank")
+            nc.tensor.matmul(degree[q][:], identity[:, : WIDTHS[q]], one[:], start=True, stop=False)
+
+        open_degree(0)
 
         nx_flipped = [held.tile([D, P], BF16, name=f"nx_flipped{k}") for k in range(NB)]
         for k in range(NB):
@@ -106,10 +110,11 @@ def tile_gnn_kernel(tc, base, target_x, neighbor_x, neighbor_y, offs, out):
 
         open_with_self_loop(0)
         similarities(0, blocks_a_bank=1)
-        similarities(1, blocks_a_bank=1)
+        similarities(1, blocks_a_bank=2)
         invert_degree(0)
         messages(0, 0)
         spread_inverse(0)
+        open_degree(1)
         invert_degree(1)
         messages(0, 1)
         for b in range(CB):

@@ -100,8 +100,8 @@ def tile_gnn_kernel(tc, base, target_x, neighbor_x, neighbor_y, offs, out):
                 nf, message = nx, self_loop[q]
             else:
                 nf, message = ny, banks.tile([P, WIDTHS[q]], F32, name=f"message{q}", tag="bank")
-            for k in range(NB):
-                nc.tensor.matmul(message[:], nf[:, k, :], sim[q][:, k, :], start=(b > 0 and k == 0), stop=(k == NB - 1))
+            for k in reversed(range(NB)):
+                nc.tensor.matmul(message[:], nf[:, k, :], sim[q][:, k, :], start=(b > 0 and k == NB - 1), stop=(k == 0))
             nc.scalar.activation(summed[q][b][:], message[:], COPY)
 
         def scatter(q, b):

@@ -35,10 +35,10 @@ def tile_gnn_kernel(tc, base, target_x, neighbor_x, neighbor_y, offs, out):
         windows = [held.tile([P, S], F32, name=f"window{b}") for b in range(CB)]
         nc.sync.dma_start(nx[:], neighbor_x.rearrange("(p k) d -> p k d", k=NB))
         nc.sync.dma_start(tx[:], target_x)
-        nc.sync.dma_start(offsets[:], offs)
-        nc.sync.dma_start(windows[0][:], base[:P, :])
         nc.sync.dma_start(ny[:], neighbor_y.rearrange("(p k) d -> p k d", k=NB))
-        nc.sync.dma_start(windows[1][:], base[P:, :])
+        nc.sync.dma_start(offsets[:], offs)
+        for b in range(CB):
+            nc.sync.dma_start(windows[b][:], base[b * P : (b + 1) * P, :])
 
         identity = held.tile([P, P], BF16, name="identity")
         make_identity(nc, identity[:])

import math

import concourse.mybir as mybir
from concourse.masks import make_identity

BF16, F32, U16 = mybir.dt.bfloat16, mybir.dt.float32, mybir.dt.uint16
EXP = mybir.ActivationFunctionType.Exp
COPY = mybir.ActivationFunctionType.Copy
MULT = mybir.AluOpType.mult

P = 128
D = 128
C = 256
NN = 512
S = 512
N = 256
NB = NN // P
CB = C // P
WIDTHS = (128, 128)
PARTS = len(WIDTHS)

FLOPS = 2 * NN * D * N + 2 * NN * C * N


def tile_gnn_kernel(tc, base, target_x, neighbor_x, neighbor_y, offs, out):
    nc = tc.nc
    with (
        tc.tile_pool(name="held", bufs=1) as held,
        tc.psum_pool(name="banks", bufs=8) as banks,
    ):
        nx = held.tile([P, NB, D], BF16, name="nx")
        ny = held.tile([P, NB, C - D], BF16, name="ny")
        tx = held.tile([D, N], BF16, name="tx")
        offsets = held.tile([P, N // 16], U16, name="offsets")
        windows = [held.tile([P, S], F32, name=f"window{b}") for b in range(CB)]
        nc.sync.dma_start(nx[:], neighbor_x.rearrange("(p k) d -> p k d", k=NB))
        nc.sync.dma_start(tx[:], target_x)
        nc.sync.dma_start(ny[:], neighbor_y.rearrange("(p k) d -> p k d", k=NB))
        nc.sync.dma_start(offsets[:], offs)
        for b in range(CB):
            nc.sync.dma_start(windows[b][:], base[b * P : (b + 1) * P, :])

        identity = held.tile([P, P], BF16, name="identity")
        make_identity(nc, identity[:])
        identity_f32 = held.tile([P, P], F32, name="identity_f32")
        nc.scalar.activation(identity_f32[:], identity[:], COPY)
        one = held.tile([P, 1], BF16, name="one")
        nc.vector.memset(one[:], 1.0)


        degree = {}

        def open_degree(q):
            degree[q] = banks.tile([WIDTHS[q], 1], F32, name=f"degree{q}", tag="bank")
            nc.tensor.matmul(degree[q][:], identity[:, : WIDTHS[q]], one[:], start=True, stop=False)

        open_degree(0)

        nx_flipped = [held.tile([D, P], BF16, name=f"nx_flipped{k}") for k in range(NB)]
        for k in range(NB):
            nx_flipped_psum = banks.tile([D, P], BF16, name="nx_flipped_psum", tag="bank")
            nc.tensor.matmul(nx_flipped_psum[:], nx[:, k, :], identity[:], start=True, stop=True)
            nc.vector.tensor_copy(nx_flipped[k][:], nx_flipped_psum[:])

        starts = [sum(WIDTHS[:q]) for q in range(PARTS)]
        columns = [slice(starts[q], starts[q] + WIDTHS[q]) for q in range(PARTS)]
        sim = [held.tile([P, NB, w], BF16, name=f"sim{q}") for q, w in enumerate(WIDTHS)]
        inverse_degree = [held.tile([P, w], F32, name=f"inverse_degree{q}") for q, w in enumerate(WIDTHS)]
        inverse_column = {}
        summed = [[held.tile([P, w], F32, name=f"summed{b}_{q}") for b in range(CB)] for q, w in enumerate(WIDTHS)]

        def similarities(q, blocks_a_bank):
            for first in range(0, NB, blocks_a_bank):
                blocks = slice(first, first + blocks_a_bank)
                dots = banks.tile([P, blocks_a_bank, WIDTHS[q]], F32, name=f"dots{first}_{q}", tag="bank")
                for i in range(blocks_a_bank):
                    nc.tensor.matmul(dots[:, i, :], nx_flipped[first + i][:], tx[:, columns[q]], start=True, stop=True)
                nc.scalar.activation(sim[q][:, blocks, :], dots[:], EXP, bias=-math.log(NN), scale=1.0 / math.sqrt(C))

        def invert_degree(q):
            for k in range(NB):
                nc.tensor.matmul(degree[q][:], sim[q][:, k, :], one[:], start=False, stop=(k == NB - 1))
            inverse_column[q] = held.tile([WIDTHS[q], 1], F32, name=f"inverse_column{q}")
            nc.vector.reciprocal(inverse_column[q][:], degree[q][:])

        def spread_inverse(q):
            w = WIDTHS[q]
            inverse_rows = banks.tile([P, w], F32, name=f"inverse_rows{q}", tag="bank")
            nc.tensor.transpose(inverse_rows[:], inverse_column[q][:].to_broadcast([w, P]), identity_f32[:w, :w])
            nc.scalar.activation(inverse_degree[q][:], inverse_rows[:], COPY)

        self_loop = {}

        def open_with_self_loop(q):
            self_loop[q] = banks.tile([P, WIDTHS[q]], F32, name=f"self_loop{q}", tag="bank")
            nc.tensor.matmul(self_loop[q][:], identity[:], tx[:, columns[q]], start=True, stop=False)

        def messages(q, b):
            if b == 0:
                nf, message = nx, self_loop[q]
            else:
                nf, message = ny, banks.tile([P, WIDTHS[q]], F32, name=f"message{q}", tag="bank")
            for k in reversed(range(NB)):
                nc.tensor.matmul(message[:], nf[:, k, :], sim[q][:, k, :], start=(b > 0 and k == NB - 1), stop=(k == 0))
            nc.scalar.activation(summed[q][b][:], message[:], COPY)

        def scatter(q, b):
            entries = offsets[:, starts[q] // 16 : (starts[q] + WIDTHS[q]) // 16]
            nc.vector.tensor_tensor(windows[b][:].indirect(entries), summed[q][b][:], inverse_degree[q][:], MULT)

        open_with_self_loop(0)
        similarities(0, blocks_a_bank=1)
        similarities(1, blocks_a_bank=2)
        invert_degree(0)
        messages(0, 0)
        spread_inverse(0)
        open_degree(1)
        invert_degree(1)
        messages(0, 1)
        for b in range(CB):
            scatter(0, b)
        open_with_self_loop(1)
        messages(1, 0)
        spread_inverse(1)
        messages(1, 1)
        for b in range(CB):
            scatter(1, b)
            nc.sync.dma_start(out[b * P : (b + 1) * P, :], windows[b][:])
